import numpy as np
import ml_dtypes


def mxq(x, axis, fmt="e4m3"):
    dtype, down = {"e4m3": (ml_dtypes.float8_e4m3fn, 7), "e5m2": (ml_dtypes.float8_e5m2, 14)}[fmt]
    v = np.moveaxis(np.asarray(x, np.float32).astype(ml_dtypes.bfloat16).astype(np.float64), axis, -1)
    blocks = v.reshape(v.shape[:-1] + (-1, 32))
    amax = np.abs(blocks).max(-1, keepdims=True)
    byte = np.maximum(np.where(amax > 0, np.frexp(amax)[1] - 1 + 127, 0) - down, 1)
    scale = np.exp2(byte - 127.0)
    codes = (blocks / scale).astype(np.float32).astype(dtype).astype(np.float64)
    return np.moveaxis((codes * scale).reshape(v.shape), -1, axis)


WIDE = False


def mx_kscale(k):
    if not WIDE:
        return np.ones(k)
    levels = np.array([10, -10, 5, -5, 0])
    a = np.random.permutation(np.resize(levels, k // 512 * 4)).reshape(k // 512, 4)
    idx = np.arange(k)
    return np.exp2(a[idx // 512, idx % 128 // 32])


BF16 = ml_dtypes.bfloat16


def bf(x):
    return np.asarray(x, np.float32).astype(BF16)


def f64(x):
    return np.asarray(x).astype(np.float64)


B, S, D, H, QL, KL, ND, VD, RD = 4, 256, 2048, 16, 512, 512, 128, 128, 128
QH = ND + RD
BASE = 10000.0


def rope(v):
    d = v.shape[-1]
    inv_freq = BASE ** (-np.arange(0, d, 2) / d)
    ang = np.arange(v.shape[1])[:, None] * inv_freq[None, :]
    cos = np.cos(ang)[None, :, None, :]
    sin = np.sin(ang)[None, :, None, :]
    v1 = v[..., 0::2]
    v2 = v[..., 1::2]
    o1 = v1 * cos - v2 * sin
    o2 = v1 * sin + v2 * cos
    return np.stack([o1, o2], axis=-1).reshape(v.shape)


def setup_inputs():
    s, t = mx_kscale(D), mx_kscale(QL)
    return {"x": bf(np.random.standard_normal((B, S, D)) * s),
            "Wqa": bf(np.random.standard_normal((D, QL)) / np.sqrt(D) / s[:, None] * t),
            "Wqb": bf(np.random.standard_normal((QL, H * QH)) / np.sqrt(QL) / t[:, None])}


def reference(x, Wqa, Wqb):
    cq = mxq(f64(x), 2, "e4m3") @ mxq(f64(Wqa), 0, "e4m3")
    q = (mxq(cq, 2, "e4m3") @ mxq(f64(Wqb), 0, "e4m3")).reshape(B, S, H, QH)
    q_nope, q_pe = q[..., :ND], q[..., ND:]
    return np.concatenate([q_nope, rope(q_pe)], axis=-1)

@@ -1,0 +1,293 @@
+import math
+from contextlib import ExitStack
+
+import concourse.mybir as mybir
+from concourse.masks import make_identity
+
+F32 = mybir.dt.float32
+BF16 = mybir.dt.bfloat16
+I32 = mybir.dt.int32
+U32 = mybir.dt.uint32
+U8 = mybir.dt.uint8
+FP8X4 = mybir.dt.float8_e4m3fn_x4
+ALU = mybir.AluOpType
+ACT = mybir.ActivationFunctionType
+
+P = 128
+PACK = 4
+K_PASS = P * PACK
+
+BATCH, SEQ, D_MODEL, HEADS, Q_RANK = 4, 256, 2048, 16, 512
+PLAIN, ROTARY = 128, 128
+HEAD = PLAIN + ROTARY
+PAIRS = ROTARY // 2
+PAIR_BITS = 6
+assert 2**PAIR_BITS == PAIRS
+ROPE_BASE = 10000.0
+
+TOKENS = BATCH * SEQ
+TOKEN_TILES = TOKENS // P
+SEQ_HALVES = SEQ // P
+D_PASSES = D_MODEL // K_PASS
+RANK_TILES = Q_RANK // P
+
+CHUNK_HEADS = 4
+CHUNKS = HEADS // CHUNK_HEADS
+CHUNK_COLS = CHUNK_HEADS * HEAD
+BANK = CHUNK_HEADS * PLAIN
+KINDS = 2
+
+FLOPS = 2 * TOKENS * D_MODEL * Q_RANK + 2 * TOKENS * Q_RANK * HEADS * HEAD
+
+TWO_PI = 2.0 * math.pi
+TWO_PI_HIGH = round(TWO_PI * 2.0**15) / 2.0**15
+TWO_PI_LOW = TWO_PI - TWO_PI_HIGH
+ROUND_MAGIC = 1.5 * 2.0**23
+
+
+def build_rotation_tables(nc, pool):
+    position_int = pool.tile([P, SEQ_HALVES], I32, name="position_int")
+    nc.gpsimd.iota(position_int[:], pattern=[[P, SEQ_HALVES]], base=0, channel_multiplier=1)
+    position = pool.tile([P, SEQ_HALVES], F32, name="position")
+    nc.vector.tensor_copy(out=position[:], in_=position_int[:])
+
+    ratio = ROPE_BASE ** (-2.0 / ROTARY)
+    frequency = pool.tile([P, PAIRS], F32, name="frequency")
+    nc.vector.memset(frequency[:, 0:1], 1.0)
+    for doubling in range(PAIR_BITS):
+        filled = 2**doubling
+        nc.vector.tensor_scalar_mul(
+            out=frequency[:, filled : 2 * filled], in0=frequency[:, 0:filled], scalar1=ratio**filled
+        )
+
+    angle = pool.tile([P, SEQ_HALVES, PAIRS], F32, name="angle")
+    for half in range(SEQ_HALVES):
+        nc.vector.tensor_scalar_mul(
+            out=angle[:, half, :], in0=frequency[:], scalar1=position[:, half : half + 1]
+        )
+
+    turns = pool.tile([P, SEQ_HALVES, PAIRS], F32, name="turns")
+    nc.vector.tensor_scalar(
+        out=turns[:], in0=angle[:], scalar1=1.0 / TWO_PI, scalar2=ROUND_MAGIC, op0=ALU.mult, op1=ALU.add
+    )
+    nc.vector.tensor_scalar_sub(out=turns[:], in0=turns[:], scalar1=ROUND_MAGIC)
+    partly = pool.tile([P, SEQ_HALVES, PAIRS], F32, name="partly")
+    nc.vector.scalar_tensor_tensor(
+        out=partly[:], in0=turns[:], scalar=-TWO_PI_HIGH, in1=angle[:], op0=ALU.mult, op1=ALU.add
+    )
+    reduced = pool.tile([P, SEQ_HALVES, PAIRS], F32, name="reduced")
+    nc.vector.scalar_tensor_tensor(
+        out=reduced[:], in0=turns[:], scalar=-TWO_PI_LOW, in1=partly[:], op0=ALU.mult, op1=ALU.add
+    )
+
+    magnitude = pool.tile([P, SEQ_HALVES, PAIRS], F32, name="magnitude")
+    nc.vector.scalar_tensor_tensor(
+        out=magnitude[:], in0=reduced[:], scalar=-1.0, in1=reduced[:], op0=ALU.mult, op1=ALU.max
+    )
+    complement = pool.tile([P, SEQ_HALVES, PAIRS], F32, name="complement")
+    nc.vector.tensor_scalar(
+        out=complement[:], in0=magnitude[:], scalar1=-0.5, scalar2=math.pi / 2.0, op0=ALU.mult, op1=ALU.add
+    )
+    sin_half = pool.tile([P, SEQ_HALVES, PAIRS], F32, name="sin_half")
+    nc.scalar.activation(out=sin_half[:], in_=reduced[:], func=ACT.Sin, scale=0.5)
+    cos_half = pool.tile([P, SEQ_HALVES, PAIRS], F32, name="cos_half")
+    nc.scalar.activation(out=cos_half[:], in_=complement[:], func=ACT.Sin)
+
+    table_u = pool.tile([P, SEQ_HALVES, PAIRS, 2], F32, name="table_u")
+    table_w = pool.tile([P, SEQ_HALVES, PAIRS, 2], F32, name="table_w")
+    nc.vector.scalar_tensor_tensor(
+        out=table_u[:, :, :, 1], in0=sin_half[:], scalar=2.0, in1=cos_half[:], op0=ALU.mult, op1=ALU.mult
+    )
+    nc.vector.scalar_tensor_tensor(
+        out=table_w[:, :, :, 0], in0=sin_half[:], scalar=-2.0, in1=cos_half[:], op0=ALU.mult, op1=ALU.mult
+    )
+    cos_less_one = pool.tile([P, SEQ_HALVES, PAIRS], F32, name="cos_less_one")
+    nc.vector.scalar_tensor_tensor(
+        out=cos_less_one[:], in0=sin_half[:], scalar=-2.0, in1=sin_half[:], op0=ALU.mult, op1=ALU.mult
+    )
+    nc.vector.tensor_scalar_add(out=table_u[:, :, :, 0], in0=cos_less_one[:], scalar1=1.0)
+    nc.vector.tensor_scalar_add(out=table_w[:, :, :, 1], in0=cos_less_one[:], scalar1=1.0)
+    return table_u, table_w
+
+
+def tile_multilatentattention_pa_kernel(tc, x, Wqa, Wqb, out):
+    nc = tc.nc
+    x_rows = x.rearrange("b s d -> (b s) d")
+    out_rows = out.rearrange("b s h f -> (b s) (h f)")
+    wqb_by_partition = Wqb.rearrange("(t p) n -> p t n", t=PACK, p=P)
+
+    with ExitStack() as ctx:
+        keep = ctx.enter_context(tc.tile_pool(name="keep", bufs=1))
+        stage = ctx.enter_context(tc.tile_pool(name="stage", bufs=3))
+        results = ctx.enter_context(tc.tile_pool(name="results", bufs=6))
+        psum = ctx.enter_context(tc.psum_pool(name="psum", bufs=2))
+
+        a_raw = keep.tile([P, D_PASSES, PACK, Q_RANK], BF16, name="a_raw")
+        x_raw = keep.tile([P, TOKEN_TILES, D_MODEL], BF16, name="x_raw")
+        b_raw = keep.tile([P, CHUNKS, PACK, CHUNK_COLS], BF16, name="b_raw")
+
+        a_codes = keep.tile([P, D_PASSES, Q_RANK], U32, name="a_codes", align_bytes=64)
+        a_scales = keep.tile([P, D_PASSES, Q_RANK], U8, name="a_scales", align_bytes=64)
+        x_codes = keep.tile([P, TOKEN_TILES, D_PASSES, P], U32, name="x_codes", align_bytes=64)
+        x_scales = keep.tile([P, TOKEN_TILES, D_PASSES, P], U8, name="x_scales", align_bytes=64)
+        cq_codes = keep.tile([P, TOKEN_TILES, P], U32, name="cq_codes", align_bytes=64)
+        cq_scales = keep.tile([P, TOKEN_TILES, P], U8, name="cq_scales", align_bytes=64)
+        b_codes = keep.tile([P, CHUNKS, KINDS, BANK], U32, name="b_codes", align_bytes=64)
+        b_scales = keep.tile([P, CHUNKS, KINDS, BANK], U8, name="b_scales", align_bytes=64)
+
+        def load_b(chunk):
+            cols = slice(chunk * CHUNK_COLS, (chunk + 1) * CHUNK_COLS)
+            nc.sync.dma_start(out=b_raw[:, chunk], in_=wqb_by_partition[:, :, cols])
+
+        def load_a(g):
+            rows = Wqa[g * K_PASS : (g + 1) * K_PASS, :]
+            nc.sync.dma_start(
+                out=a_raw[:, g].rearrange("p (u e) n -> p u (e n)", u=2),
+                in_=rows.rearrange("(u q e) n -> q u (e n)", u=2, q=P, e=2),
+            )
+
+        def load_x(i):
+            nc.sync.dma_start(out=x_raw[:, i, :], in_=x_rows[i * P : (i + 1) * P, :])
+
+        load_b(0)
+        for g in range(D_PASSES):
+            load_a(g)
+        for i in range(TOKEN_TILES):
+            load_x(i)
+        for chunk in range(1, CHUNKS):
+            load_b(chunk)
+
+        identity = keep.tile([P, P], F32, name="identity")
+        make_identity(nc, identity[:])
+        table_u, table_w = build_rotation_tables(nc, keep)
+
+        b_grouped = {}
+
+        def regroup_b(chunk, piece):
+            kind, head = divmod(piece, CHUNK_HEADS)
+            if head == 0:
+                b_grouped[(chunk, kind)] = stage.tile(
+                    [P, BANK, PACK], BF16, name="b_grouped", tag="b_grouped", align_bytes=64
+                )
+            first = head * HEAD + kind * PLAIN
+            nc.scalar.copy(
+                out=b_grouped[(chunk, kind)][:, head * PLAIN : (head + 1) * PLAIN, :].rearrange(
+                    "p (c i) t -> p c t i", i=4
+                ),
+                in_=b_raw[:, chunk, :, first : first + PLAIN].rearrange("p t (c i) -> p c t i", i=4),
+            )
+            if head == CHUNK_HEADS - 1:
+                nc.vector.quantize_mx(
+                    out=b_codes[:, chunk, kind, :].bitcast(FP8X4),
+                    scales=b_scales[:, chunk, kind, :],
+                    in_=b_grouped[(chunk, kind)][:].rearrange("p n t -> p (n t)"),
+                )
+
+        for piece in range(KINDS * CHUNK_HEADS):
+            regroup_b(0, piece)
+
+        for g in range(D_PASSES):
+            a_grouped = stage.tile([P, Q_RANK, PACK], BF16, name="a_grouped", align_bytes=64)
+            nc.vector.tensor_copy(
+                out=a_grouped[:].rearrange("p (c i) t -> p c t i", i=4),
+                in_=a_raw[:, g].rearrange("p t (c i) -> p c t i", i=4),
+            )
+            nc.vector.quantize_mx(
+                out=a_codes[:, g, :].bitcast(FP8X4),
+                scales=a_scales[:, g, :],
+                in_=a_grouped[:].rearrange("p n t -> p (n t)"),
+            )
+
+        def quantise_x(i):
+            x_words = x_raw[:, i, :].bitcast(F32)
+            x_grouped = stage.tile([P, D_PASSES * P * PACK], BF16, name="x_grouped", align_bytes=64)
+            grouped_words = x_grouped[:].bitcast(F32).rearrange("p (g r u) -> p g r u", g=D_PASSES, r=P, u=2)
+            passes_per_bank = 2
+            for first_pass in range(0, D_PASSES, passes_per_bank):
+                turned = psum.tile([P, passes_per_bank * 2, P], F32, name="turned")
+                for c in range(passes_per_bank * 2):
+                    block = first_pass * 2 + c
+                    nc.tensor.transpose(turned[:, c, :], x_words[:, block * P : (block + 1) * P], identity[:])
+                nc.scalar.copy(
+                    out=grouped_words[:, first_pass : first_pass + passes_per_bank],
+                    in_=turned[:].rearrange("p (g u) r -> p g r u", u=2),
+                )
+            nc.vector.quantize_mx(
+                out=x_codes[:, i].rearrange("p g r -> p (g r)").bitcast(FP8X4),
+                scales=x_scales[:, i].rearrange("p g r -> p (g r)"),
+                in_=x_grouped[:],
+            )
+
+        def first_product(i):
+            cq_bank = psum.tile([P, RANK_TILES, P], F32, name="cq_bank")
+            for t in range(RANK_TILES):
+                for g in range(D_PASSES):
+                    nc.tensor.matmul_mx(
+                        out=cq_bank[:, t, :],
+                        lhsT=a_codes[:, g, t * P : (t + 1) * P].bitcast(FP8X4),
+                        lhsT_scale=a_scales[:, g, t * P : (t + 1) * P],
+                        rhs=x_codes[:, i, g, :].bitcast(FP8X4),
+                        rhs_scale=x_scales[:, i, g, :],
+                        start=(g == 0),
+                        stop=(g == D_PASSES - 1),
+                    )
+            cq_grouped = stage.tile([P, P, PACK], BF16, name="cq_grouped", align_bytes=64)
+            nc.scalar.copy(out=cq_grouped[:], in_=cq_bank[:].rearrange("p t r -> p r t"))
+            nc.vector.quantize_mx(
+                out=cq_codes[:, i, :].bitcast(FP8X4),
+                scales=cq_scales[:, i, :],
+                in_=cq_grouped[:].rearrange("p r t -> p (r t)"),
+            )
+
+        def second_product(i, chunk):
+            banks = []
+            for kind in range(KINDS):
+                bank = psum.tile([P, BANK], F32, name="bank%d" % kind)
+                nc.tensor.matmul_mx(
+                    out=bank[:],
+                    lhsT=cq_codes[:, i, :].bitcast(FP8X4),
+                    lhsT_scale=cq_scales[:, i, :],
+                    rhs=b_codes[:, chunk, kind, :].bitcast(FP8X4),
+                    rhs_scale=b_scales[:, chunk, kind, :],
+                    start=True,
+                    stop=True,
+                )
+                banks.append(bank)
+            heads = results.tile([P, CHUNK_HEADS, HEAD], F32, name="heads")
+            nc.scalar.copy(
+                out=heads[:, :, 0:PLAIN], in_=banks[0][:].rearrange("p (h f) -> p h f", h=CHUNK_HEADS)
+            )
+            pairs = banks[1][:].rearrange("p (h j e) -> p h j e", h=CHUNK_HEADS, j=PAIRS, e=2)
+            shape = [P, CHUNK_HEADS, PAIRS, 2]
+            half = i % SEQ_HALVES
+            rotated = heads[:, :, PLAIN:HEAD]
+            nc.vector.tensor_tensor(
+                out=rotated.rearrange("p h (j e) -> p h j e", e=2),
+                in0=pairs[:, :, :, 0:1].to_broadcast(shape),
+                in1=table_u[:, half : half + 1].to_broadcast(shape),
+                op=ALU.mult,
+            )
+            w_part = results.tile([P, CHUNK_HEADS, ROTARY], F32, name="w_part")
+            nc.vector.tensor_tensor(
+                out=w_part[:].rearrange("p h (j e) -> p h j e", e=2),
+                in0=pairs[:, :, :, 1:2].to_broadcast(shape),
+                in1=table_w[:, half : half + 1].to_broadcast(shape),
+                op=ALU.mult,
+            )
+            nc.gpsimd.tensor_tensor(out=rotated, in0=rotated, in1=w_part[:], op=ALU.add)
+            nc.sync.dma_start(
+                out=out_rows[i * P : (i + 1) * P, chunk * CHUNK_COLS : (chunk + 1) * CHUNK_COLS],
+                in_=heads[:].rearrange("p h f -> p (h f)"),
+            )
+
+        for i in range(TOKEN_TILES):
+            quantise_x(i)
+            first_product(i)
+            second_product(i, 0)
+            regroup_b(1, i)
+
+        for chunk in range(1, CHUNKS):
+            for i in range(TOKEN_TILES):
+                second_product(i, chunk)
+                if chunk + 1 < CHUNKS:
+                    regroup_b(chunk + 1, i)

@@ -37,6 +37,9 @@ CHUNK_COLS = CHUNK_HEADS * HEAD
 BANK = CHUNK_HEADS * PLAIN
 KINDS = 2
 
+LAG = 2
+AHEAD = 4
+
 FLOPS = 2 * TOKENS * D_MODEL * Q_RANK + 2 * TOKENS * Q_RANK * HEADS * HEAD
 
 TWO_PI = 2.0 * math.pi
@@ -121,6 +124,7 @@ def tile_multilatentattention_pa_kernel(tc, x, Wqa, Wqb, out):
         stage = ctx.enter_context(tc.tile_pool(name="stage", bufs=3))
         results = ctx.enter_context(tc.tile_pool(name="results", bufs=6))
         psum = ctx.enter_context(tc.psum_pool(name="psum", bufs=2))
+        ctx.enter_context(tc.manual_schedule())
 
         a_raw = keep.tile([P, D_PASSES, PACK, Q_RANK], BF16, name="a_raw")
         x_raw = keep.tile([P, TOKEN_TILES, D_MODEL], BF16, name="x_raw")
@@ -152,9 +156,12 @@ def tile_multilatentattention_pa_kernel(tc, x, Wqa, Wqb, out):
         load_b(0)
         for g in range(D_PASSES):
             load_a(g)
-        for i in range(TOKEN_TILES):
+        for i in range(TOKEN_TILES // 2):
             load_x(i)
-        for chunk in range(1, CHUNKS):
+        load_b(1)
+        for i in range(TOKEN_TILES // 2, TOKEN_TILES):
+            load_x(i)
+        for chunk in range(2, CHUNKS):
             load_b(chunk)
 
         identity = keep.tile([P, P], F32, name="identity")
@@ -163,39 +170,48 @@ def tile_multilatentattention_pa_kernel(tc, x, Wqa, Wqb, out):
 
         b_grouped = {}
 
-        def regroup_b(chunk, piece):
-            kind, head = divmod(piece, CHUNK_HEADS)
-            if head == 0:
+        def regroup_b(copy, chunk, kind, first_head, heads):
+            if first_head == 0:
                 b_grouped[(chunk, kind)] = stage.tile(
                     [P, BANK, PACK], BF16, name="b_grouped", tag="b_grouped", align_bytes=64
                 )
-            first = head * HEAD + kind * PLAIN
-            nc.scalar.copy(
-                out=b_grouped[(chunk, kind)][:, head * PLAIN : (head + 1) * PLAIN, :].rearrange(
-                    "p (c i) t -> p c t i", i=4
-                ),
-                in_=b_raw[:, chunk, :, first : first + PLAIN].rearrange("p t (c i) -> p c t i", i=4),
+            some = slice(first_head, first_head + heads)
+            copy(
+                out=b_grouped[(chunk, kind)][:].rearrange(
+                    "p (h c i) t -> p h c t i", h=CHUNK_HEADS, i=4
+                )[:, some],
+                in_=b_raw[:, chunk].rearrange(
+                    "p t (h k c i) -> p k h c t i", h=CHUNK_HEADS, k=KINDS, i=4
+                )[:, kind, some],
             )
+
+        def quantise_b(chunk, kind):
+            nc.vector.quantize_mx(
+                out=b_codes[:, chunk, kind, :].bitcast(FP8X4),
+                scales=b_scales[:, chunk, kind, :],
+                in_=b_grouped[(chunk, kind)][:].rearrange("p n t -> p (n t)"),
+            )
+
+        def regroup_b_on_scalar(chunk, piece):
+            kind, head = divmod(piece, CHUNK_HEADS)
+            regroup_b(nc.scalar.copy, chunk, kind, head, 1)
             if head == CHUNK_HEADS - 1:
-                nc.vector.quantize_mx(
-                    out=b_codes[:, chunk, kind, :].bitcast(FP8X4),
-                    scales=b_scales[:, chunk, kind, :],
-                    in_=b_grouped[(chunk, kind)][:].rearrange("p n t -> p (n t)"),
-                )
+                quantise_b(chunk, kind)
 
-        for piece in range(KINDS * CHUNK_HEADS):
-            regroup_b(0, piece)
+        a_grouped = {}
 
-        for g in range(D_PASSES):
-            a_grouped = stage.tile([P, Q_RANK, PACK], BF16, name="a_grouped", align_bytes=64)
+        def regroup_a(g):
+            a_grouped[g] = stage.tile([P, Q_RANK, PACK], BF16, name="a_grouped", tag="a_grouped", align_bytes=64)
             nc.vector.tensor_copy(
-                out=a_grouped[:].rearrange("p (c i) t -> p c t i", i=4),
+                out=a_grouped[g][:].rearrange("p (c i) t -> p c t i", i=4),
                 in_=a_raw[:, g].rearrange("p t (c i) -> p c t i", i=4),
             )
+
+        def quantise_a(g):
             nc.vector.quantize_mx(
                 out=a_codes[:, g, :].bitcast(FP8X4),
                 scales=a_scales[:, g, :],
-                in_=a_grouped[:].rearrange("p n t -> p (n t)"),
+                in_=a_grouped[g][:].rearrange("p n t -> p (n t)"),
             )
 
         def quantise_x(i):
@@ -280,14 +296,39 @@ def tile_multilatentattention_pa_kernel(tc, x, Wqa, Wqb, out):
                 in_=heads[:].rearrange("p h f -> p (h f)"),
             )
 
-        for i in range(TOKEN_TILES):
-            quantise_x(i)
-            first_product(i)
-            second_product(i, 0)
-            regroup_b(1, i)
+        for g in range(D_PASSES + 1):
+            if g < D_PASSES:
+                regroup_a(g)
+            if g > 0:
+                quantise_a(g - 1)
+        for piece in range(KINDS * CHUNK_HEADS):
+            regroup_b_on_scalar(0, piece)
 
+        vector_jobs = [
+            lambda: regroup_b(nc.vector.tensor_copy, 1, 0, 0, CHUNK_HEADS),
+            lambda: regroup_b(nc.vector.tensor_copy, 1, 1, 0, CHUNK_HEADS),
+            lambda: quantise_b(1, 0),
+            lambda: quantise_b(1, 1),
+        ]
+        for step in range(TOKEN_TILES + 2 * LAG):
+            if step < TOKEN_TILES:
+                quantise_x(step)
+            if LAG <= step < TOKEN_TILES + LAG:
+                first_product(step - LAG)
+            if step >= 2 * LAG:
+                second_product(step - 2 * LAG, 0)
+            if LAG <= step < LAG + len(vector_jobs):
+                vector_jobs[step - LAG]()
+
+        late_pieces = [
+            (chunk, piece) for chunk in range(2, CHUNKS) for piece in range(KINDS * CHUNK_HEADS)
+        ]
+        for chunk, piece in late_pieces[:AHEAD]:
+            regroup_b_on_scalar(chunk, piece)
+        turn = 0
         for chunk in range(1, CHUNKS):
             for i in range(TOKEN_TILES):
                 second_product(i, chunk)
-                if chunk + 1 < CHUNKS:
-                    regroup_b(chunk + 1, i)
+                if AHEAD + turn < len(late_pieces):
+                    regroup_b_on_scalar(*late_pieces[AHEAD + turn])
+                turn += 1

@@ -37,8 +37,10 @@ CHUNK_COLS = CHUNK_HEADS * HEAD
 BANK = CHUNK_HEADS * PLAIN
 KINDS = 2
 
+WAVE_CHUNKS = 2
 LAG = 2
 AHEAD = 4
+PSUM_BANKS = 8
 
 FLOPS = 2 * TOKENS * D_MODEL * Q_RANK + 2 * TOKENS * Q_RANK * HEADS * HEAD
 
@@ -123,7 +125,7 @@ def tile_multilatentattention_pa_kernel(tc, x, Wqa, Wqb, out):
         keep = ctx.enter_context(tc.tile_pool(name="keep", bufs=1))
         stage = ctx.enter_context(tc.tile_pool(name="stage", bufs=3))
         results = ctx.enter_context(tc.tile_pool(name="results", bufs=6))
-        psum = ctx.enter_context(tc.psum_pool(name="psum", bufs=2))
+        psum = ctx.enter_context(tc.psum_pool(name="psum", bufs=PSUM_BANKS))
         ctx.enter_context(tc.manual_schedule())
 
         a_raw = keep.tile([P, D_PASSES, PACK, Q_RANK], BF16, name="a_raw")
@@ -156,10 +158,10 @@ def tile_multilatentattention_pa_kernel(tc, x, Wqa, Wqb, out):
         load_b(0)
         for g in range(D_PASSES):
             load_a(g)
-        for i in range(TOKEN_TILES // 2):
+        for i in range(LAG):
             load_x(i)
         load_b(1)
-        for i in range(TOKEN_TILES // 2, TOKEN_TILES):
+        for i in range(LAG, TOKEN_TILES):
             load_x(i)
         for chunk in range(2, CHUNKS):
             load_b(chunk)
@@ -220,7 +222,7 @@ def tile_multilatentattention_pa_kernel(tc, x, Wqa, Wqb, out):
             grouped_words = x_grouped[:].bitcast(F32).rearrange("p (g r u) -> p g r u", g=D_PASSES, r=P, u=2)
             passes_per_bank = 2
             for first_pass in range(0, D_PASSES, passes_per_bank):
-                turned = psum.tile([P, passes_per_bank * 2, P], F32, name="turned")
+                turned = psum.tile([P, passes_per_bank * 2, P], F32, name="turned", tag="bank")
                 for c in range(passes_per_bank * 2):
                     block = first_pass * 2 + c
                     nc.tensor.transpose(turned[:, c, :], x_words[:, block * P : (block + 1) * P], identity[:])
@@ -235,7 +237,7 @@ def tile_multilatentattention_pa_kernel(tc, x, Wqa, Wqb, out):
             )
 
         def first_product(i):
-            cq_bank = psum.tile([P, RANK_TILES, P], F32, name="cq_bank")
+            cq_bank = psum.tile([P, RANK_TILES, P], F32, name="cq_bank", tag="bank")
             for t in range(RANK_TILES):
                 for g in range(D_PASSES):
                     nc.tensor.matmul_mx(
@@ -258,7 +260,7 @@ def tile_multilatentattention_pa_kernel(tc, x, Wqa, Wqb, out):
         def second_product(i, chunk):
             banks = []
             for kind in range(KINDS):
-                bank = psum.tile([P, BANK], F32, name="bank%d" % kind)
+                bank = psum.tile([P, BANK], F32, name="bank", tag="bank")
                 nc.tensor.matmul_mx(
                     out=bank[:],
                     lhsT=cq_codes[:, i, :].bitcast(FP8X4),
@@ -310,25 +312,33 @@ def tile_multilatentattention_pa_kernel(tc, x, Wqa, Wqb, out):
             lambda: quantise_b(1, 0),
             lambda: quantise_b(1, 1),
         ]
-        for step in range(TOKEN_TILES + 2 * LAG):
+        late_pieces = [
+            (chunk, piece) for chunk in range(WAVE_CHUNKS, CHUNKS) for piece in range(KINDS * CHUNK_HEADS)
+        ]
+        regrouped = []
+
+        def regroup_next():
+            if len(regrouped) < len(late_pieces):
+                regroup_b_on_scalar(*late_pieces[len(regrouped)])
+                regrouped.append(True)
+
+        for step in range(TOKEN_TILES + LAG + WAVE_CHUNKS):
             if step < TOKEN_TILES:
                 quantise_x(step)
             if LAG <= step < TOKEN_TILES + LAG:
                 first_product(step - LAG)
-            if step >= 2 * LAG:
-                second_product(step - 2 * LAG, 0)
-            if LAG <= step < LAG + len(vector_jobs):
-                vector_jobs[step - LAG]()
+            for chunk in range(WAVE_CHUNKS):
+                i = step - LAG - 1 - chunk
+                if 0 <= i < TOKEN_TILES:
+                    second_product(i, chunk)
+            if step < len(vector_jobs):
+                vector_jobs[step]()
+            else:
+                regroup_next()
 
-        late_pieces = [
-            (chunk, piece) for chunk in range(2, CHUNKS) for piece in range(KINDS * CHUNK_HEADS)
-        ]
-        for chunk, piece in late_pieces[:AHEAD]:
-            regroup_b_on_scalar(chunk, piece)
-        turn = 0
-        for chunk in range(1, CHUNKS):
+        for extra in range(AHEAD):
+            regroup_next()
+        for chunk in range(WAVE_CHUNKS, CHUNKS):
             for i in range(TOKEN_TILES):
                 second_product(i, chunk)
-                if AHEAD + turn < len(late_pieces):
-                    regroup_b_on_scalar(*late_pieces[AHEAD + turn])
-                turn += 1
+                regroup_next()

@@ -40,6 +40,7 @@ KINDS = 2
 WAVE_CHUNKS = 2
 LAG = 2
 AHEAD = 4
+VECTOR_ADDS = 4
 PSUM_BANKS = 8
 
 FLOPS = 2 * TOKENS * D_MODEL * Q_RANK + 2 * TOKENS * Q_RANK * HEADS * HEAD
@@ -98,21 +99,20 @@ def build_rotation_tables(nc, pool):
     cos_half = pool.tile([P, SEQ_HALVES, PAIRS], F32, name="cos_half")
     nc.scalar.activation(out=cos_half[:], in_=complement[:], func=ACT.Sin)
 
-    table_u = pool.tile([P, SEQ_HALVES, PAIRS, 2], F32, name="table_u")
-    table_w = pool.tile([P, SEQ_HALVES, PAIRS, 2], F32, name="table_w")
+    table = pool.tile([P, 2, SEQ_HALVES, PAIRS, 2], F32, name="table")
     nc.vector.scalar_tensor_tensor(
-        out=table_u[:, :, :, 1], in0=sin_half[:], scalar=2.0, in1=cos_half[:], op0=ALU.mult, op1=ALU.mult
+        out=table[:, 0, :, :, 1], in0=sin_half[:], scalar=2.0, in1=cos_half[:], op0=ALU.mult, op1=ALU.mult
     )
     nc.vector.scalar_tensor_tensor(
-        out=table_w[:, :, :, 0], in0=sin_half[:], scalar=-2.0, in1=cos_half[:], op0=ALU.mult, op1=ALU.mult
+        out=table[:, 1, :, :, 0], in0=sin_half[:], scalar=-2.0, in1=cos_half[:], op0=ALU.mult, op1=ALU.mult
     )
     cos_less_one = pool.tile([P, SEQ_HALVES, PAIRS], F32, name="cos_less_one")
     nc.vector.scalar_tensor_tensor(
         out=cos_less_one[:], in0=sin_half[:], scalar=-2.0, in1=sin_half[:], op0=ALU.mult, op1=ALU.mult
     )
-    nc.vector.tensor_scalar_add(out=table_u[:, :, :, 0], in0=cos_less_one[:], scalar1=1.0)
-    nc.vector.tensor_scalar_add(out=table_w[:, :, :, 1], in0=cos_less_one[:], scalar1=1.0)
-    return table_u, table_w
+    nc.vector.tensor_scalar_add(out=table[:, 0, :, :, 0], in0=cos_less_one[:], scalar1=1.0)
+    nc.vector.tensor_scalar_add(out=table[:, 1, :, :, 1], in0=cos_less_one[:], scalar1=1.0)
+    return table
 
 
 def tile_multilatentattention_pa_kernel(tc, x, Wqa, Wqb, out):
@@ -168,7 +168,7 @@ def tile_multilatentattention_pa_kernel(tc, x, Wqa, Wqb, out):
 
         identity = keep.tile([P, P], F32, name="identity")
         make_identity(nc, identity[:])
-        table_u, table_w = build_rotation_tables(nc, keep)
+        table = build_rotation_tables(nc, keep)
 
         b_grouped = {}
 
@@ -275,24 +275,28 @@ def tile_multilatentattention_pa_kernel(tc, x, Wqa, Wqb, out):
             nc.scalar.copy(
                 out=heads[:, :, 0:PLAIN], in_=banks[0][:].rearrange("p (h f) -> p h f", h=CHUNK_HEADS)
             )
-            pairs = banks[1][:].rearrange("p (h j e) -> p h j e", h=CHUNK_HEADS, j=PAIRS, e=2)
-            shape = [P, CHUNK_HEADS, PAIRS, 2]
-            half = i % SEQ_HALVES
-            rotated = heads[:, :, PLAIN:HEAD]
+            shape = [P, 2, CHUNK_HEADS, PAIRS, 2]
+            products = results.tile([P, 2, CHUNK_HEADS, ROTARY], F32, name="products")
             nc.vector.tensor_tensor(
-                out=rotated.rearrange("p h (j e) -> p h j e", e=2),
-                in0=pairs[:, :, :, 0:1].to_broadcast(shape),
-                in1=table_u[:, half : half + 1].to_broadcast(shape),
+                out=products[:].rearrange("p x h (j e) -> p x h j e", e=2),
+                in0=banks[1][:]
+                .rearrange("p (h j x) -> p x h j", h=CHUNK_HEADS, j=PAIRS, x=2)
+                .unsqueeze(4)
+                .to_broadcast(shape),
+                in1=table[:, :, i % SEQ_HALVES].unsqueeze(2).to_broadcast(shape),
                 op=ALU.mult,
             )
-            w_part = results.tile([P, CHUNK_HEADS, ROTARY], F32, name="w_part")
-            nc.vector.tensor_tensor(
-                out=w_part[:].rearrange("p h (j e) -> p h j e", e=2),
-                in0=pairs[:, :, :, 1:2].to_broadcast(shape),
-                in1=table_w[:, half : half + 1].to_broadcast(shape),
-                op=ALU.mult,
+            if unfinished:
+                add_and_store(*unfinished[-1])
+            unfinished.append((i, chunk, heads, products))
+
+        unfinished = []
+
+        def add_and_store(i, chunk, heads, products):
+            adder = nc.vector if i % VECTOR_ADDS == VECTOR_ADDS - 1 else nc.gpsimd
+            adder.tensor_tensor(
+                out=heads[:, :, PLAIN:HEAD], in0=products[:, 0], in1=products[:, 1], op=ALU.add
             )
-            nc.gpsimd.tensor_tensor(out=rotated, in0=rotated, in1=w_part[:], op=ALU.add)
             nc.sync.dma_start(
                 out=out_rows[i * P : (i + 1) * P, chunk * CHUNK_COLS : (chunk + 1) * CHUNK_COLS],
                 in_=heads[:].rearrange("p h f -> p (h f)"),
@@ -342,3 +346,4 @@ def tile_multilatentattention_pa_kernel(tc, x, Wqa, Wqb, out):
             for i in range(TOKEN_TILES):
                 second_product(i, chunk)
                 regroup_next()
+        add_and_store(*unfinished[-1])

@@ -35,11 +35,14 @@ CHUNK_HEADS = 4
 CHUNKS = HEADS // CHUNK_HEADS
 CHUNK_COLS = CHUNK_HEADS * HEAD
 BANK = CHUNK_HEADS * PLAIN
+CHUNK_PAIRS = CHUNK_HEADS * PAIRS
 KINDS = 2
+PLAIN_KIND, ROTARY_KIND = 0, 1
 
-WAVE_CHUNKS = 2
 LAG = 2
-AHEAD = 4
+CHUNK_LAG = 3
+PREPARE_STEPS = 4
+VECTOR_CHUNKS = 2
 VECTOR_ADDS = 4
 PSUM_BANKS = 8
 
@@ -99,20 +102,24 @@ def build_rotation_tables(nc, pool):
     cos_half = pool.tile([P, SEQ_HALVES, PAIRS], F32, name="cos_half")
     nc.scalar.activation(out=cos_half[:], in_=complement[:], func=ACT.Sin)
 
-    table = pool.tile([P, 2, SEQ_HALVES, PAIRS, 2], F32, name="table")
+    sine = pool.tile([P, SEQ_HALVES, PAIRS], F32, name="sine")
     nc.vector.scalar_tensor_tensor(
-        out=table[:, 0, :, :, 1], in0=sin_half[:], scalar=2.0, in1=cos_half[:], op0=ALU.mult, op1=ALU.mult
-    )
-    nc.vector.scalar_tensor_tensor(
-        out=table[:, 1, :, :, 0], in0=sin_half[:], scalar=-2.0, in1=cos_half[:], op0=ALU.mult, op1=ALU.mult
+        out=sine[:], in0=sin_half[:], scalar=2.0, in1=cos_half[:], op0=ALU.mult, op1=ALU.mult
     )
     cos_less_one = pool.tile([P, SEQ_HALVES, PAIRS], F32, name="cos_less_one")
     nc.vector.scalar_tensor_tensor(
         out=cos_less_one[:], in0=sin_half[:], scalar=-2.0, in1=sin_half[:], op0=ALU.mult, op1=ALU.mult
     )
-    nc.vector.tensor_scalar_add(out=table[:, 0, :, :, 0], in0=cos_less_one[:], scalar1=1.0)
-    nc.vector.tensor_scalar_add(out=table[:, 1, :, :, 1], in0=cos_less_one[:], scalar1=1.0)
-    return table
+    cosine = pool.tile([P, SEQ_HALVES, PAIRS], F32, name="cosine")
+    nc.vector.tensor_scalar_add(out=cosine[:], in0=cos_less_one[:], scalar1=1.0)
+    mixed = pool.tile([P, SEQ_HALVES, PAIRS, 2], F32, name="mixed")
+    nc.vector.scalar_tensor_tensor(
+        out=mixed[:, :, :, 0], in0=cosine[:], scalar=-1.0, in1=sine[:], op0=ALU.mult, op1=ALU.subtract
+    )
+    nc.vector.scalar_tensor_tensor(
+        out=mixed[:, :, :, 1], in0=cosine[:], scalar=-1.0, in1=sine[:], op0=ALU.mult, op1=ALU.add
+    )
+    return cosine, mixed
 
 
 def tile_multilatentattention_pa_kernel(tc, x, Wqa, Wqb, out):
@@ -155,20 +162,18 @@ def tile_multilatentattention_pa_kernel(tc, x, Wqa, Wqb, out):
         def load_x(i):
             nc.sync.dma_start(out=x_raw[:, i, :], in_=x_rows[i * P : (i + 1) * P, :])
 
+        tiles_per_chunk = TOKEN_TILES // CHUNKS
         load_b(0)
         for g in range(D_PASSES):
             load_a(g)
-        for i in range(LAG):
+        for i in range(TOKEN_TILES):
+            if i > 0 and i % tiles_per_chunk == 0:
+                load_b(i // tiles_per_chunk)
             load_x(i)
-        load_b(1)
-        for i in range(LAG, TOKEN_TILES):
-            load_x(i)
-        for chunk in range(2, CHUNKS):
-            load_b(chunk)
 
         identity = keep.tile([P, P], F32, name="identity")
         make_identity(nc, identity[:])
-        table = build_rotation_tables(nc, keep)
+        cosine, mixed = build_rotation_tables(nc, keep)
 
         b_grouped = {}
 
@@ -178,14 +183,24 @@ def tile_multilatentattention_pa_kernel(tc, x, Wqa, Wqb, out):
                     [P, BANK, PACK], BF16, name="b_grouped", tag="b_grouped", align_bytes=64
                 )
             some = slice(first_head, first_head + heads)
-            copy(
-                out=b_grouped[(chunk, kind)][:].rearrange(
-                    "p (h c i) t -> p h c t i", h=CHUNK_HEADS, i=4
-                )[:, some],
-                in_=b_raw[:, chunk].rearrange(
-                    "p t (h k c i) -> p k h c t i", h=CHUNK_HEADS, k=KINDS, i=4
-                )[:, kind, some],
-            )
+            grouped = b_grouped[(chunk, kind)]
+            if kind == PLAIN_KIND:
+                copy(
+                    out=grouped[:].rearrange("p (h c i) t -> p h c t i", h=CHUNK_HEADS, i=4)[:, some],
+                    in_=b_raw[:, chunk].rearrange(
+                        "p t (h k c i) -> p k h c t i", h=CHUNK_HEADS, k=KINDS, i=4
+                    )[:, PLAIN_KIND, some],
+                )
+            else:
+                for block in range(2):
+                    copy(
+                        out=grouped[:].rearrange(
+                            "p (b h c i) t -> p b h c t i", b=2, h=CHUNK_HEADS, i=4
+                        )[:, block, some],
+                        in_=b_raw[:, chunk].rearrange(
+                            "p t (h k c i e) -> p k e h c t i", h=CHUNK_HEADS, k=KINDS, i=4, e=2
+                        )[:, ROTARY_KIND, 1 - block, some],
+                    )
 
         def quantise_b(chunk, kind):
             nc.vector.quantize_mx(
@@ -194,11 +209,18 @@ def tile_multilatentattention_pa_kernel(tc, x, Wqa, Wqb, out):
                 in_=b_grouped[(chunk, kind)][:].rearrange("p n t -> p (n t)"),
             )
 
-        def regroup_b_on_scalar(chunk, piece):
-            kind, head = divmod(piece, CHUNK_HEADS)
-            regroup_b(nc.scalar.copy, chunk, kind, head, 1)
-            if head == CHUNK_HEADS - 1:
-                quantise_b(chunk, kind)
+        def prepare_b(chunk, part):
+            if 1 <= chunk <= VECTOR_CHUNKS:
+                if part < KINDS:
+                    regroup_b(nc.vector.tensor_copy, chunk, KINDS - 1 - part, 0, CHUNK_HEADS)
+                else:
+                    quantise_b(chunk, 2 * KINDS - 1 - part)
+            else:
+                for kind in (ROTARY_KIND, PLAIN_KIND):
+                    regroup_b(nc.scalar.copy, chunk, kind, part, 1)
+                if part == CHUNK_HEADS - 1:
+                    for kind in (ROTARY_KIND, PLAIN_KIND):
+                        quantise_b(chunk, kind)
 
         a_grouped = {}
 
@@ -257,45 +279,58 @@ def tile_multilatentattention_pa_kernel(tc, x, Wqa, Wqb, out):
                 in_=cq_grouped[:].rearrange("p r t -> p (r t)"),
             )
 
-        def second_product(i, chunk):
-            banks = []
-            for kind in range(KINDS):
-                bank = psum.tile([P, BANK], F32, name="bank", tag="bank")
-                nc.tensor.matmul_mx(
-                    out=bank[:],
-                    lhsT=cq_codes[:, i, :].bitcast(FP8X4),
-                    lhsT_scale=cq_scales[:, i, :],
-                    rhs=b_codes[:, chunk, kind, :].bitcast(FP8X4),
-                    rhs_scale=b_scales[:, chunk, kind, :],
-                    start=True,
-                    stop=True,
-                )
-                banks.append(bank)
-            heads = results.tile([P, CHUNK_HEADS, HEAD], F32, name="heads")
-            nc.scalar.copy(
-                out=heads[:, :, 0:PLAIN], in_=banks[0][:].rearrange("p (h f) -> p h f", h=CHUNK_HEADS)
+        def second_pass(i, bank, chunk, kind, cols, start, stop):
+            nc.tensor.matmul_mx(
+                out=bank,
+                lhsT=cq_codes[:, i, :].bitcast(FP8X4),
+                lhsT_scale=cq_scales[:, i, :],
+                rhs=b_codes[:, chunk, kind, cols].bitcast(FP8X4),
+                rhs_scale=b_scales[:, chunk, kind, cols],
+                start=start,
+                stop=stop,
             )
-            shape = [P, 2, CHUNK_HEADS, PAIRS, 2]
-            products = results.tile([P, 2, CHUNK_HEADS, ROTARY], F32, name="products")
-            nc.vector.tensor_tensor(
-                out=products[:].rearrange("p x h (j e) -> p x h j e", e=2),
-                in0=banks[1][:]
-                .rearrange("p (h j x) -> p x h j", h=CHUNK_HEADS, j=PAIRS, x=2)
-                .unsqueeze(4)
-                .to_broadcast(shape),
-                in1=table[:, :, i % SEQ_HALVES].unsqueeze(2).to_broadcast(shape),
-                op=ALU.mult,
-            )
-            if unfinished:
-                add_and_store(*unfinished[-1])
-            unfinished.append((i, chunk, heads, products))
 
         unfinished = []
 
-        def add_and_store(i, chunk, heads, products):
+        def second_product(i, chunk):
+            w_then_u = psum.tile([P, 2, CHUNK_PAIRS], F32, name="w_then_u", tag="bank")
+            second_pass(i, w_then_u[:].rearrange("p b n -> p (b n)"), chunk, ROTARY_KIND, slice(0, BANK), True, True)
+            u_plus_w = psum.tile([P, CHUNK_PAIRS], F32, name="u_plus_w", tag="bank")
+            second_pass(i, u_plus_w[:], chunk, ROTARY_KIND, slice(0, CHUNK_PAIRS), True, False)
+            second_pass(i, u_plus_w[:], chunk, ROTARY_KIND, slice(CHUNK_PAIRS, BANK), False, True)
+            plain = psum.tile([P, BANK], F32, name="plain", tag="bank")
+            second_pass(i, plain[:], chunk, PLAIN_KIND, slice(0, BANK), True, True)
+
+            half = i % SEQ_HALVES
+            heads = results.tile([P, CHUNK_HEADS, HEAD], F32, name="heads")
+            nc.vector.tensor_tensor(
+                out=heads[:, :, PLAIN:HEAD].rearrange("p h (j e) -> p h j e", e=2),
+                in0=w_then_u[:].rearrange("p b (h j) -> p h j b", h=CHUNK_HEADS),
+                in1=mixed[:, half].unsqueeze(1).to_broadcast([P, CHUNK_HEADS, PAIRS, 2]),
+                op=ALU.mult,
+            )
+            shared = results.tile([P, CHUNK_HEADS, PAIRS], F32, name="shared")
+            nc.vector.tensor_tensor(
+                out=shared[:],
+                in0=u_plus_w[:].rearrange("p (h j) -> p h j", h=CHUNK_HEADS),
+                in1=cosine[:, half].unsqueeze(1).to_broadcast([P, CHUNK_HEADS, PAIRS]),
+                op=ALU.mult,
+            )
+            nc.scalar.copy(
+                out=heads[:, :, 0:PLAIN], in_=plain[:].rearrange("p (h f) -> p h f", h=CHUNK_HEADS)
+            )
+            if unfinished:
+                add_and_store(*unfinished[-1])
+            unfinished.append((i, chunk, heads, shared))
+
+        def add_and_store(i, chunk, heads, shared):
             adder = nc.vector if i % VECTOR_ADDS == VECTOR_ADDS - 1 else nc.gpsimd
+            rotated = heads[:, :, PLAIN:HEAD].rearrange("p h (j e) -> p h j e", e=2)
             adder.tensor_tensor(
-                out=heads[:, :, PLAIN:HEAD], in0=products[:, 0], in1=products[:, 1], op=ALU.add
+                out=rotated,
+                in0=rotated,
+                in1=shared[:].unsqueeze(3).to_broadcast([P, CHUNK_HEADS, PAIRS, 2]),
+                op=ALU.add,
             )
             nc.sync.dma_start(
                 out=out_rows[i * P : (i + 1) * P, chunk * CHUNK_COLS : (chunk + 1) * CHUNK_COLS],
@@ -307,43 +342,19 @@ def tile_multilatentattention_pa_kernel(tc, x, Wqa, Wqb, out):
                 regroup_a(g)
             if g > 0:
                 quantise_a(g - 1)
-        for piece in range(KINDS * CHUNK_HEADS):
-            regroup_b_on_scalar(0, piece)
+        for part in range(PREPARE_STEPS):
+            prepare_b(0, part)
 
-        vector_jobs = [
-            lambda: regroup_b(nc.vector.tensor_copy, 1, 0, 0, CHUNK_HEADS),
-            lambda: regroup_b(nc.vector.tensor_copy, 1, 1, 0, CHUNK_HEADS),
-            lambda: quantise_b(1, 0),
-            lambda: quantise_b(1, 1),
-        ]
-        late_pieces = [
-            (chunk, piece) for chunk in range(WAVE_CHUNKS, CHUNKS) for piece in range(KINDS * CHUNK_HEADS)
-        ]
-        regrouped = []
-
-        def regroup_next():
-            if len(regrouped) < len(late_pieces):
-                regroup_b_on_scalar(*late_pieces[len(regrouped)])
-                regrouped.append(True)
-
-        for step in range(TOKEN_TILES + LAG + WAVE_CHUNKS):
+        assert PREPARE_STEPS * (CHUNKS - 1) <= LAG + 1 + CHUNK_LAG * (CHUNKS - 1)
+        for step in range(TOKEN_TILES + LAG + 1 + CHUNK_LAG * (CHUNKS - 1)):
             if step < TOKEN_TILES:
                 quantise_x(step)
             if LAG <= step < TOKEN_TILES + LAG:
                 first_product(step - LAG)
-            for chunk in range(WAVE_CHUNKS):
-                i = step - LAG - 1 - chunk
+            if step < PREPARE_STEPS * (CHUNKS - 1):
+                prepare_b(1 + step // PREPARE_STEPS, step % PREPARE_STEPS)
+            for chunk in range(CHUNKS):
+                i = step - LAG - 1 - CHUNK_LAG * chunk
                 if 0 <= i < TOKEN_TILES:
                     second_product(i, chunk)
-            if step < len(vector_jobs):
-                vector_jobs[step]()
-            else:
-                regroup_next()
-
-        for extra in range(AHEAD):
-            regroup_next()
-        for chunk in range(WAVE_CHUNKS, CHUNKS):
-            for i in range(TOKEN_TILES):
-                second_product(i, chunk)
-                regroup_next()
         add_and_store(*unfinished[-1])

import math
from contextlib import ExitStack

import concourse.mybir as mybir
from concourse.masks import make_identity

F32 = mybir.dt.float32
BF16 = mybir.dt.bfloat16
I32 = mybir.dt.int32
U32 = mybir.dt.uint32
U8 = mybir.dt.uint8
FP8X4 = mybir.dt.float8_e4m3fn_x4
ALU = mybir.AluOpType
ACT = mybir.ActivationFunctionType

P = 128
PACK = 4
K_PASS = P * PACK

BATCH, SEQ, D_MODEL, HEADS, Q_RANK = 4, 256, 2048, 16, 512
PLAIN, ROTARY = 128, 128
HEAD = PLAIN + ROTARY
PAIRS = ROTARY // 2
PAIR_BITS = 6
assert 2**PAIR_BITS == PAIRS
ROPE_BASE = 10000.0

TOKENS = BATCH * SEQ
TOKEN_TILES = TOKENS // P
SEQ_HALVES = SEQ // P
D_PASSES = D_MODEL // K_PASS
RANK_TILES = Q_RANK // P

CHUNK_HEADS = 4
CHUNKS = HEADS // CHUNK_HEADS
CHUNK_COLS = CHUNK_HEADS * HEAD
BANK = CHUNK_HEADS * PLAIN
CHUNK_PAIRS = CHUNK_HEADS * PAIRS
KINDS = 2
PLAIN_KIND, ROTARY_KIND = 0, 1

LAG = 2
CHUNK_LAG = 3
PREPARE_STEPS = 4
VECTOR_CHUNKS = 2
VECTOR_ADDS = 4
PSUM_BANKS = 8

FLOPS = 2 * TOKENS * D_MODEL * Q_RANK + 2 * TOKENS * Q_RANK * HEADS * HEAD

TWO_PI = 2.0 * math.pi
TWO_PI_HIGH = round(TWO_PI * 2.0**15) / 2.0**15
TWO_PI_LOW = TWO_PI - TWO_PI_HIGH
ROUND_MAGIC = 1.5 * 2.0**23


def build_rotation_tables(nc, pool):
    position_int = pool.tile([P, SEQ_HALVES], I32, name="position_int")
    nc.gpsimd.iota(position_int[:], pattern=[[P, SEQ_HALVES]], base=0, channel_multiplier=1)
    position = pool.tile([P, SEQ_HALVES], F32, name="position")
    nc.vector.tensor_copy(out=position[:], in_=position_int[:])

    ratio = ROPE_BASE ** (-2.0 / ROTARY)
    frequency = pool.tile([P, PAIRS], F32, name="frequency")
    nc.vector.memset(frequency[:, 0:1], 1.0)
    for doubling in range(PAIR_BITS):
        filled = 2**doubling
        nc.vector.tensor_scalar_mul(
            out=frequency[:, filled : 2 * filled], in0=frequency[:, 0:filled], scalar1=ratio**filled
        )

    angle = pool.tile([P, SEQ_HALVES, PAIRS], F32, name="angle")
    for half in range(SEQ_HALVES):
        nc.vector.tensor_scalar_mul(
            out=angle[:, half, :], in0=frequency[:], scalar1=position[:, half : half + 1]
        )

    turns = pool.tile([P, SEQ_HALVES, PAIRS], F32, name="turns")
    nc.vector.tensor_scalar(
        out=turns[:], in0=angle[:], scalar1=1.0 / TWO_PI, scalar2=ROUND_MAGIC, op0=ALU.mult, op1=ALU.add
    )
    nc.vector.tensor_scalar_sub(out=turns[:], in0=turns[:], scalar1=ROUND_MAGIC)
    partly = pool.tile([P, SEQ_HALVES, PAIRS], F32, name="partly")
    nc.vector.scalar_tensor_tensor(
        out=partly[:], in0=turns[:], scalar=-TWO_PI_HIGH, in1=angle[:], op0=ALU.mult, op1=ALU.add
    )
    reduced = pool.tile([P, SEQ_HALVES, PAIRS], F32, name="reduced")
    nc.vector.scalar_tensor_tensor(
        out=reduced[:], in0=turns[:], scalar=-TWO_PI_LOW, in1=partly[:], op0=ALU.mult, op1=ALU.add
    )

    magnitude = pool.tile([P, SEQ_HALVES, PAIRS], F32, name="magnitude")
    nc.vector.scalar_tensor_tensor(
        out=magnitude[:], in0=reduced[:], scalar=-1.0, in1=reduced[:], op0=ALU.mult, op1=ALU.max
    )
    complement = pool.tile([P, SEQ_HALVES, PAIRS], F32, name="complement")
    nc.vector.tensor_scalar(
        out=complement[:], in0=magnitude[:], scalar1=-0.5, scalar2=math.pi / 2.0, op0=ALU.mult, op1=ALU.add
    )
    sin_half = pool.tile([P, SEQ_HALVES, PAIRS], F32, name="sin_half")
    nc.scalar.activation(out=sin_half[:], in_=reduced[:], func=ACT.Sin, scale=0.5)
    cos_half = pool.tile([P, SEQ_HALVES, PAIRS], F32, name="cos_half")
    nc.scalar.activation(out=cos_half[:], in_=complement[:], func=ACT.Sin)

    sine = pool.tile([P, SEQ_HALVES, PAIRS], F32, name="sine")
    nc.vector.scalar_tensor_tensor(
        out=sine[:], in0=sin_half[:], scalar=2.0, in1=cos_half[:], op0=ALU.mult, op1=ALU.mult
    )
    cos_less_one = pool.tile([P, SEQ_HALVES, PAIRS], F32, name="cos_less_one")
    nc.vector.scalar_tensor_tensor(
        out=cos_less_one[:], in0=sin_half[:], scalar=-2.0, in1=sin_half[:], op0=ALU.mult, op1=ALU.mult
    )
    cosine = pool.tile([P, SEQ_HALVES, PAIRS], F32, name="cosine")
    nc.vector.tensor_scalar_add(out=cosine[:], in0=cos_less_one[:], scalar1=1.0)
    mixed = pool.tile([P, SEQ_HALVES, PAIRS, 2], F32, name="mixed")
    nc.vector.scalar_tensor_tensor(
        out=mixed[:, :, :, 0], in0=cosine[:], scalar=-1.0, in1=sine[:], op0=ALU.mult, op1=ALU.subtract
    )
    nc.vector.scalar_tensor_tensor(
        out=mixed[:, :, :, 1], in0=cosine[:], scalar=-1.0, in1=sine[:], op0=ALU.mult, op1=ALU.add
    )
    return cosine, mixed


def tile_multilatentattention_pa_kernel(tc, x, Wqa, Wqb, out):
    nc = tc.nc
    x_rows = x.rearrange("b s d -> (b s) d")
    out_rows = out.rearrange("b s h f -> (b s) (h f)")
    wqb_by_partition = Wqb.rearrange("(t p) n -> p t n", t=PACK, p=P)

    with ExitStack() as ctx:
        keep = ctx.enter_context(tc.tile_pool(name="keep", bufs=1))
        stage = ctx.enter_context(tc.tile_pool(name="stage", bufs=3))
        results = ctx.enter_context(tc.tile_pool(name="results", bufs=6))
        psum = ctx.enter_context(tc.psum_pool(name="psum", bufs=PSUM_BANKS))
        ctx.enter_context(tc.manual_schedule())

        a_raw = keep.tile([P, D_PASSES, PACK, Q_RANK], BF16, name="a_raw")
        x_raw = keep.tile([P, TOKEN_TILES, D_MODEL], BF16, name="x_raw")
        b_raw = keep.tile([P, CHUNKS, PACK, CHUNK_COLS], BF16, name="b_raw")

        a_codes = keep.tile([P, D_PASSES, Q_RANK], U32, name="a_codes", align_bytes=64)
        a_scales = keep.tile([P, D_PASSES, Q_RANK], U8, name="a_scales", align_bytes=64)
        x_codes = keep.tile([P, TOKEN_TILES, D_PASSES, P], U32, name="x_codes", align_bytes=64)
        x_scales = keep.tile([P, TOKEN_TILES, D_PASSES, P], U8, name="x_scales", align_bytes=64)
        cq_codes = keep.tile([P, TOKEN_TILES, P], U32, name="cq_codes", align_bytes=64)
        cq_scales = keep.tile([P, TOKEN_TILES, P], U8, name="cq_scales", align_bytes=64)
        b_codes = keep.tile([P, CHUNKS, KINDS, BANK], U32, name="b_codes", align_bytes=64)
        b_scales = keep.tile([P, CHUNKS, KINDS, BANK], U8, name="b_scales", align_bytes=64)

        def load_b(chunk):
            cols = slice(chunk * CHUNK_COLS, (chunk + 1) * CHUNK_COLS)
            nc.sync.dma_start(out=b_raw[:, chunk], in_=wqb_by_partition[:, :, cols])

        def load_a(g):
            rows = Wqa[g * K_PASS : (g + 1) * K_PASS, :]
            nc.sync.dma_start(
                out=a_raw[:, g].rearrange("p (u e) n -> p u (e n)", u=2),
                in_=rows.rearrange("(u q e) n -> q u (e n)", u=2, q=P, e=2),
            )

        def load_x(i):
            nc.sync.dma_start(out=x_raw[:, i, :], in_=x_rows[i * P : (i + 1) * P, :])

        tiles_per_chunk = TOKEN_TILES // CHUNKS
        load_b(0)
        for g in range(D_PASSES):
            load_a(g)
        for i in range(TOKEN_TILES):
            if i > 0 and i % tiles_per_chunk == 0:
                load_b(i // tiles_per_chunk)
            load_x(i)

        identity = keep.tile([P, P], F32, name="identity")
        make_identity(nc, identity[:])
        cosine, mixed = build_rotation_tables(nc, keep)

        b_grouped = {}

        def regroup_b(copy, chunk, kind, first_head, heads):
            if first_head == 0:
                b_grouped[(chunk, kind)] = stage.tile(
                    [P, BANK, PACK], BF16, name="b_grouped", tag="b_grouped", align_bytes=64
                )
            some = slice(first_head, first_head + heads)
            grouped = b_grouped[(chunk, kind)]
            if kind == PLAIN_KIND:
                copy(
                    out=grouped[:].rearrange("p (h c i) t -> p h c t i", h=CHUNK_HEADS, i=4)[:, some],
                    in_=b_raw[:, chunk].rearrange(
                        "p t (h k c i) -> p k h c t i", h=CHUNK_HEADS, k=KINDS, i=4
                    )[:, PLAIN_KIND, some],
                )
            else:
                for block in range(2):
                    copy(
                        out=grouped[:].rearrange(
                            "p (b h c i) t -> p b h c t i", b=2, h=CHUNK_HEADS, i=4
                        )[:, block, some],
                        in_=b_raw[:, chunk].rearrange(
                            "p t (h k c i e) -> p k e h c t i", h=CHUNK_HEADS, k=KINDS, i=4, e=2
                        )[:, ROTARY_KIND, 1 - block, some],
                    )

        def quantise_b(chunk, kind):
            nc.vector.quantize_mx(
                out=b_codes[:, chunk, kind, :].bitcast(FP8X4),
                scales=b_scales[:, chunk, kind, :],
                in_=b_grouped[(chunk, kind)][:].rearrange("p n t -> p (n t)"),
            )

        def prepare_b(chunk, part):
            if 1 <= chunk <= VECTOR_CHUNKS:
                if part < KINDS:
                    regroup_b(nc.vector.tensor_copy, chunk, KINDS - 1 - part, 0, CHUNK_HEADS)
                else:
                    quantise_b(chunk, 2 * KINDS - 1 - part)
            else:
                for kind in (ROTARY_KIND, PLAIN_KIND):
                    regroup_b(nc.scalar.copy, chunk, kind, part, 1)
                if part == CHUNK_HEADS - 1:
                    for kind in (ROTARY_KIND, PLAIN_KIND):
                        quantise_b(chunk, kind)

        a_grouped = {}

        def regroup_a(g):
            a_grouped[g] = stage.tile([P, Q_RANK, PACK], BF16, name="a_grouped", tag="a_grouped", align_bytes=64)
            nc.vector.tensor_copy(
                out=a_grouped[g][:].rearrange("p (c i) t -> p c t i", i=4),
                in_=a_raw[:, g].rearrange("p t (c i) -> p c t i", i=4),
            )

        def quantise_a(g):
            nc.vector.quantize_mx(
                out=a_codes[:, g, :].bitcast(FP8X4),
                scales=a_scales[:, g, :],
                in_=a_grouped[g][:].rearrange("p n t -> p (n t)"),
            )

        def quantise_x(i):
            x_words = x_raw[:, i, :].bitcast(F32)
            x_grouped = stage.tile([P, D_PASSES * P * PACK], BF16, name="x_grouped", align_bytes=64)
            grouped_words = x_grouped[:].bitcast(F32).rearrange("p (g r u) -> p g r u", g=D_PASSES, r=P, u=2)
            passes_per_bank = 2
            for first_pass in range(0, D_PASSES, passes_per_bank):
                turned = psum.tile([P, passes_per_bank * 2, P], F32, name="turned", tag="bank")
                for c in range(passes_per_bank * 2):
                    block = first_pass * 2 + c
                    nc.tensor.transpose(turned[:, c, :], x_words[:, block * P : (block + 1) * P], identity[:])
                nc.scalar.copy(
                    out=grouped_words[:, first_pass : first_pass + passes_per_bank],
                    in_=turned[:].rearrange("p (g u) r -> p g r u", u=2),
                )
            nc.vector.quantize_mx(
                out=x_codes[:, i].rearrange("p g r -> p (g r)").bitcast(FP8X4),
                scales=x_scales[:, i].rearrange("p g r -> p (g r)"),
                in_=x_grouped[:],
            )

        def first_product(i):
            cq_bank = psum.tile([P, RANK_TILES, P], F32, name="cq_bank", tag="bank")
            for t in range(RANK_TILES):
                for g in range(D_PASSES):
                    nc.tensor.matmul_mx(
                        out=cq_bank[:, t, :],
                        lhsT=a_codes[:, g, t * P : (t + 1) * P].bitcast(FP8X4),
                        lhsT_scale=a_scales[:, g, t * P : (t + 1) * P],
                        rhs=x_codes[:, i, g, :].bitcast(FP8X4),
                        rhs_scale=x_scales[:, i, g, :],
                        start=(g == 0),
                        stop=(g == D_PASSES - 1),
                    )
            cq_grouped = stage.tile([P, P, PACK], BF16, name="cq_grouped", align_bytes=64)
            nc.scalar.copy(out=cq_grouped[:], in_=cq_bank[:].rearrange("p t r -> p r t"))
            nc.vector.quantize_mx(
                out=cq_codes[:, i, :].bitcast(FP8X4),
                scales=cq_scales[:, i, :],
                in_=cq_grouped[:].rearrange("p r t -> p (r t)"),
            )

        def second_pass(i, bank, chunk, kind, cols, start, stop):
            nc.tensor.matmul_mx(
                out=bank,
                lhsT=cq_codes[:, i, :].bitcast(FP8X4),
                lhsT_scale=cq_scales[:, i, :],
                rhs=b_codes[:, chunk, kind, cols].bitcast(FP8X4),
                rhs_scale=b_scales[:, chunk, kind, cols],
                start=start,
                stop=stop,
            )

        unfinished = []

        def second_product(i, chunk):
            w_then_u = psum.tile([P, 2, CHUNK_PAIRS], F32, name="w_then_u", tag="bank")
            second_pass(i, w_then_u[:].rearrange("p b n -> p (b n)"), chunk, ROTARY_KIND, slice(0, BANK), True, True)
            u_plus_w = psum.tile([P, CHUNK_PAIRS], F32, name="u_plus_w", tag="bank")
            second_pass(i, u_plus_w[:], chunk, ROTARY_KIND, slice(0, CHUNK_PAIRS), True, False)
            second_pass(i, u_plus_w[:], chunk, ROTARY_KIND, slice(CHUNK_PAIRS, BANK), False, True)
            plain = psum.tile([P, BANK], F32, name="plain", tag="bank")
            second_pass(i, plain[:], chunk, PLAIN_KIND, slice(0, BANK), True, True)

            half = i % SEQ_HALVES
            heads = results.tile([P, CHUNK_HEADS, HEAD], F32, name="heads")
            nc.vector.tensor_tensor(
                out=heads[:, :, PLAIN:HEAD].rearrange("p h (j e) -> p h j e", e=2),
                in0=w_then_u[:].rearrange("p b (h j) -> p h j b", h=CHUNK_HEADS),
                in1=mixed[:, half].unsqueeze(1).to_broadcast([P, CHUNK_HEADS, PAIRS, 2]),
                op=ALU.mult,
            )
            shared = results.tile([P, CHUNK_HEADS, PAIRS], F32, name="shared")
            nc.vector.tensor_tensor(
                out=shared[:],
                in0=u_plus_w[:].rearrange("p (h j) -> p h j", h=CHUNK_HEADS),
                in1=cosine[:, half].unsqueeze(1).to_broadcast([P, CHUNK_HEADS, PAIRS]),
                op=ALU.mult,
            )
            nc.scalar.copy(
                out=heads[:, :, 0:PLAIN], in_=plain[:].rearrange("p (h f) -> p h f", h=CHUNK_HEADS)
            )
            if unfinished:
                add_and_store(*unfinished[-1])
            unfinished.append((i, chunk, heads, shared))

        def add_and_store(i, chunk, heads, shared):
            adder = nc.vector if i % VECTOR_ADDS == VECTOR_ADDS - 1 else nc.gpsimd
            rotated = heads[:, :, PLAIN:HEAD].rearrange("p h (j e) -> p h j e", e=2)
            adder.tensor_tensor(
                out=rotated,
                in0=rotated,
                in1=shared[:].unsqueeze(3).to_broadcast([P, CHUNK_HEADS, PAIRS, 2]),
                op=ALU.add,
            )
            nc.sync.dma_start(
                out=out_rows[i * P : (i + 1) * P, chunk * CHUNK_COLS : (chunk + 1) * CHUNK_COLS],
                in_=heads[:].rearrange("p h f -> p (h f)"),
            )

        for g in range(D_PASSES + 1):
            if g < D_PASSES:
                regroup_a(g)
            if g > 0:
                quantise_a(g - 1)
        for part in range(PREPARE_STEPS):
            prepare_b(0, part)

        assert PREPARE_STEPS * (CHUNKS - 1) <= LAG + 1 + CHUNK_LAG * (CHUNKS - 1)
        for step in range(TOKEN_TILES + LAG + 1 + CHUNK_LAG * (CHUNKS - 1)):
            if step < TOKEN_TILES:
                quantise_x(step)
            if LAG <= step < TOKEN_TILES + LAG:
                first_product(step - LAG)
            if step < PREPARE_STEPS * (CHUNKS - 1):
                prepare_b(1 + step // PREPARE_STEPS, step % PREPARE_STEPS)
            for chunk in range(CHUNKS):
                i = step - LAG - 1 - CHUNK_LAG * chunk
                if 0 <= i < TOKEN_TILES:
                    second_product(i, chunk)
        add_and_store(*unfinished[-1])
